import numpy as np
import ml_dtypes


def mxq(x, axis, fmt="e4m3"):
    dtype, down = {"e4m3": (ml_dtypes.float8_e4m3fn, 7), "e5m2": (ml_dtypes.float8_e5m2, 14)}[fmt]
    v = np.moveaxis(np.asarray(x, np.float32).astype(ml_dtypes.bfloat16).astype(np.float64), axis, -1)
    blocks = v.reshape(v.shape[:-1] + (-1, 32))
    amax = np.abs(blocks).max(-1, keepdims=True)
    byte = np.maximum(np.where(amax > 0, np.frexp(amax)[1] - 1 + 127, 0) - down, 1)
    scale = np.exp2(byte - 127.0)
    codes = (blocks / scale).astype(np.float32).astype(dtype).astype(np.float64)
    return np.moveaxis((codes * scale).reshape(v.shape), -1, axis)


WIDE = False


def mx_kscale(k):
    if not WIDE:
        return np.ones(k)
    levels = np.array([10, -10, 5, -5, 0])
    if k % 512:
        return np.exp2(np.random.permutation(np.resize(levels, k // 32))).repeat(32)
    a = np.empty((k // 512, 16))
    for p in range(k // 512):
        a[p, :8] = np.random.permutation(np.resize(levels, 8))
        for g in range(8):
            far = levels[np.abs(levels - a[p, g]) >= 10]
            a[p, g + 8] = far[np.random.randint(len(far))]
    return np.exp2(a.ravel()).repeat(32)


BF16 = ml_dtypes.bfloat16


def bf(x):
    return np.asarray(x, np.float32).astype(BF16)


def f64(x):
    return np.asarray(x).astype(np.float64)


B, W, U, H, D, K, MAX_BACK, MAX_FWD = 2, 8, 256, 1, 1024, 512, 255, 0
CH = H * D
F = MAX_BACK + MAX_FWD + 1


def draw0():
    s, t = mx_kscale(CH), mx_kscale(D)
    a = 1.5 * D ** -0.25
    return {"queries": bf(np.random.standard_normal((B, W, U, H, D)) * a * t),
            "keys": bf(np.random.standard_normal((B, W, K, H, D)) * a / t),
            "sin_emb": bf(np.random.standard_normal((F, CH)) * np.sqrt(0.5) * s),
            "pos_w": bf(np.random.standard_normal((CH, CH)) * 2.0 * D ** -0.25 / np.sqrt(CH) / s[None, :] / np.tile(t, H)[:, None])}


def relative_shift(x):
    pad = K + 1 - F
    x = np.pad(x, ((0, 0), (0, 0), (0, 0), (0, 0), (0, pad)))
    x = x.reshape(B, H, W, U * (K + 1))[:, :, :, : U * K]
    return x.reshape(B, H, W, U, K)


def core(queries, keys, sin_emb, pos_w):
    proj = (mxq(f64(sin_emb), 1, "e4m3") @ mxq(f64(pos_w), 1, "e4m3").T).reshape(F, H, D)
    qq = mxq(f64(queries), 4, "e4m3").transpose(0, 3, 1, 2, 4)
    kq = mxq(f64(keys), 4, "e4m3").transpose(0, 3, 1, 4, 2)
    pq = mxq(proj, 2, "e4m3").transpose(1, 2, 0)[None, :, None]
    term_ac = qq @ kq
    term_bd = qq @ pq
    return term_ac + relative_shift(term_bd)


def e4m3fn_bytes(y):
    return np.clip(np.asarray(y, np.float64), -448.0, 448.0).astype(np.float32).astype(ml_dtypes.float8_e4m3fn).view(np.uint8)


def e4m3fn_values(b):
    return np.asarray(b, np.uint8).view(ml_dtypes.float8_e4m3fn).astype(np.float64)


def setup_inputs():
    d = draw0()
    x0 = np.asarray(d['keys']).astype(np.float64)
    s = (np.max(np.abs(x0), axis=(0, 1, 2, 3), keepdims=True) / 448.0).astype(np.float32)
    out = {}
    for k, v in d.items():
        if k == 'keys':
            out['keys_bytes'] = e4m3fn_bytes(x0 / s.astype(np.float64))
            out['keys_scale'] = s
        else:
            out[k] = v
    return out


def reference(queries, keys_bytes, keys_scale, sin_emb, pos_w):
    return core(queries, e4m3fn_values(keys_bytes) * keys_scale.astype(np.float64), sin_emb, pos_w)

@@ -1,0 +1,345 @@
+from contextlib import ExitStack
+
+import concourse.mybir as mybir
+from concourse.masks import make_identity
+
+B, W, U, D, K, F = 2, 8, 256, 1024, 512, 256
+FLOPS = 2 * (B * W * U * K * D + B * W * U * F * D + F * D * D)
+
+F32 = mybir.dt.float32
+BF16 = mybir.dt.bfloat16
+U32 = mybir.dt.uint32
+U8 = mybir.dt.uint8
+FP8 = mybir.dt.float8_e4m3fn
+FP8X4 = mybir.dt.float8_e4m3fn_x4
+ADD = mybir.AluOpType.add
+MULT = mybir.AluOpType.mult
+
+P = 128
+NB = B * W
+NSCR = 3
+WIN = 384
+AC_LAG = 2
+ADD_LAG = 3
+
+
+def tile_gemma3naudiorelativepositionembedding_pa_t_kernel(
+    tc, queries, keys_bytes, keys_scale, sin_emb, pos_w, out
+):
+    nc = tc.nc
+
+    def blk(n):
+        return n // W, n % W
+
+    with ExitStack() as ctx:
+        keep = ctx.enter_context(tc.tile_pool(name="keep", bufs=1))
+        pool = ctx.enter_context(tc.tile_pool(name="pool", bufs=3))
+        psum = ctx.enter_context(tc.psum_pool(name="psum", bufs=1))
+
+        ident = keep.tile([P, P], F32, name="ident")
+        make_identity(nc, ident[:])
+        zeros = keep.tile([P, 2, F], F32, name="zeros")
+        nc.gpsimd.memset(zeros[:], 0.0)
+        scale = keep.tile([P, D], F32, name="scale")
+        w_raw = keep.tile([P, 8 * D], BF16, name="w_raw")
+        w_grp = keep.tile([P, 8 * D], BF16, name="w_grp", align_bytes=64)
+        w_cod = keep.tile([P, 4 * 512], U32, name="w_cod", align_bytes=64)
+        w_scl = keep.tile([P, 4 * 512], U8, name="w_scl", align_bytes=64)
+        s_raw = keep.tile([P, 2 * D], BF16, name="s_raw")
+        s_grp = keep.tile([P, 2 * D], BF16, name="s_grp", align_bytes=64)
+        s_cod = keep.tile([P, 512], U32, name="s_cod", align_bytes=64)
+        s_scl = keep.tile([P, 512], U8, name="s_scl", align_bytes=64)
+        p_grp = keep.tile([P, 2 * D], BF16, name="p_grp", align_bytes=64)
+        p_cod = keep.tile([P, 512], U32, name="p_cod", align_bytes=64)
+        p_scl = keep.tile([P, 512], U8, name="p_scl", align_bytes=64)
+
+        kbytes, kval, kgrp, kcod, kscl = {}, {}, {}, {}, {}
+        qraw, qgrp, qcod, qscl = {}, {}, {}, {}
+        bank, acb, bdb, bds, shf, res = {}, {}, {}, {}, {}, {}
+
+        def load_k(n):
+            b, w = blk(n)
+            kbytes[n] = pool.tile([P, 4 * D], U8, name="kbytes", bufs=3)
+            nc.sync.dma_start(
+                out=kbytes[n][:],
+                in_=keys_bytes[b, w].rearrange("(p i) h k -> p (i h k)", i=4),
+            )
+
+        def load_q(n):
+            b, w = blk(n)
+            qraw[n] = pool.tile([P, 2 * D], BF16, name="qraw", bufs=3)
+            nc.sync.dma_start(
+                out=qraw[n][:].rearrange("p (m k) -> p m k", m=2),
+                in_=queries[b, w].rearrange("(m p) h k -> p m (h k)", p=P),
+            )
+
+        def load_w(c):
+            g, t0 = c // 2, 2 * (c % 2)
+            nc.sync.dma_start(
+                out=w_raw[:, c * 2 * D : (c + 1) * 2 * D].rearrange("m (t k) -> m t k", t=2),
+                in_=pos_w[512 * g : 512 * (g + 1), :].rearrange("(m t) k -> m t k", t=4)[:, t0 : t0 + 2, :],
+            )
+
+        def transp(key, src, base, j):
+            words = src.bitcast(F32)
+            for g in range(2):
+                if j == 0:
+                    bank[key, g] = psum.tile([P, 2, 2, P], F32, name="tp", bufs=4)
+                for u in range(2):
+                    w0 = base // 2 + 256 * g
+                    nc.tensor.transpose(
+                        bank[key, g][:, j, u, :], words[:, w0 + u : w0 + 256 : 2], ident[:]
+                    )
+
+        def copy_out(key, g, dst):
+            nc.scalar.copy(
+                out=dst.bitcast(F32).rearrange("p (j r u) -> p j r u", j=2, u=2),
+                in_=bank.pop((key, g))[:].rearrange("p j u r -> p j r u"),
+            )
+
+        def quant(cod, scl, grp):
+            nc.vector.quantize_mx(out=cod.bitcast(FP8X4), scales=scl, in_=grp)
+
+        def do_sin():
+            transp("s", s_raw[:], 0, 0)
+            transp("s", s_raw[:], D, 1)
+            for g in range(2):
+                copy_out("s", g, s_grp[:, g * D : (g + 1) * D])
+
+        def do_w(c):
+            transp("w", w_raw[:], c * 2 * D, 0)
+            transp("w", w_raw[:], c * 2 * D + D, 1)
+            for g in range(2):
+                copy_out("w", g, w_grp[:, (2 * c + g) * D : (2 * c + g + 1) * D])
+
+        def quant_w(c):
+            quant(
+                w_cod[:, 512 * c : 512 * (c + 1)],
+                w_scl[:, 512 * c : 512 * (c + 1)],
+                w_grp[:, 2 * D * c : 2 * D * (c + 1)],
+            )
+
+        def proj(G, fh):
+            pb = psum.tile([P, 4, P], F32, name="ac", bufs=3)
+            for t in range(4):
+                c = 2 * G + t // 2
+                for g in range(2):
+                    l0 = 512 * c + 256 * g + P * (t % 2)
+                    r0 = 256 * g + P * fh
+                    nc.tensor.matmul_mx(
+                        out=pb[:, t, :],
+                        lhsT=w_cod[:, l0 : l0 + P].bitcast(FP8X4),
+                        lhsT_scale=w_scl[:, l0 : l0 + P],
+                        rhs=s_cod[:, r0 : r0 + P].bitcast(FP8X4),
+                        rhs_scale=s_scl[:, r0 : r0 + P],
+                        start=(g == 0),
+                        stop=(g == 1),
+                    )
+            d0 = (2 * G + fh) * 512
+            nc.scalar.copy(
+                out=p_grp[:, d0 : d0 + 512].rearrange("p (f t) -> p f t", t=4),
+                in_=pb[:].rearrange("p t f -> p f t"),
+            )
+
+        def prod(n, i):
+            if i == 0:
+                kval[n] = pool.tile([P, 4 * D], BF16, name="kval", bufs=3)
+            cols = slice(i * D, (i + 1) * D)
+            nc.vector.tensor_tensor(
+                out=kval[n][:, cols], in0=kbytes[n][:, cols].bitcast(FP8), in1=scale[:], op=MULT
+            )
+
+        def transp_k(n, i):
+            transp(("k", n, i // 2), kval[n][:], i * D, i % 2)
+
+        def copy_k(n, pair):
+            if pair == 0:
+                kgrp[n] = pool.tile([P, 4 * D], BF16, name="kgrp", bufs=2, align_bytes=64)
+            for g in range(2):
+                d0 = (2 * g + pair) * D
+                copy_out(("k", n, pair), g, kgrp[n][:, d0 : d0 + D])
+
+        def quant_k(n, g):
+            if g == 0:
+                kcod[n] = pool.tile([P, 2 * K], U32, name="kcod", bufs=3, align_bytes=64)
+                kscl[n] = pool.tile([P, 2 * K], U8, name="kscl", bufs=3, align_bytes=64)
+            c = slice(g * K, (g + 1) * K)
+            quant(kcod[n][:, c], kscl[n][:, c], kgrp[n][:, 2 * D * g : 2 * D * (g + 1)])
+
+        def transp_q(n):
+            transp(("q", n), qraw[n][:], 0, 0)
+            transp(("q", n), qraw[n][:], D, 1)
+            qgrp[n] = pool.tile([P, 2 * D], BF16, name="qgrp", bufs=3, align_bytes=64)
+            for g in range(2):
+                copy_out(("q", n), g, qgrp[n][:, g * D : (g + 1) * D])
+
+        def quant_q(n):
+            qcod[n] = pool.tile([P, 512], U32, name="qcod", bufs=4, align_bytes=64)
+            qscl[n] = pool.tile([P, 512], U8, name="qscl", bufs=4, align_bytes=64)
+            quant(qcod[n][:], qscl[n][:], qgrp[n][:])
+
+        def mm(dst, n, m, cod, scl, width):
+            for g in range(2):
+                l0 = 256 * g + P * m
+                r = slice(width * g, width * (g + 1))
+                nc.tensor.matmul_mx(
+                    out=dst,
+                    lhsT=qcod[n][:, l0 : l0 + P].bitcast(FP8X4),
+                    lhsT_scale=qscl[n][:, l0 : l0 + P],
+                    rhs=cod[:, r].bitcast(FP8X4),
+                    rhs_scale=scl[:, r],
+                    start=(g == 0),
+                    stop=(g == 1),
+                )
+
+        def region(n):
+            b, w = blk(NB - 1 - (NB - 1 - n) % NSCR)
+            return out[b, 0, w]
+
+        def mm_bd(n):
+            bdb[n] = psum.tile([P, 2, F], F32, name="bd", bufs=1)
+            for m in range(2):
+                mm(bdb[n][:, m, :], n, m, p_cod, p_scl, F)
+            bds[n] = pool.tile([P, 2, F], F32, name="bds", bufs=3)
+            nc.scalar.copy(out=bds[n][:], in_=bdb[n][:])
+
+        def park(n):
+            nc.sync.dma_start(
+                out=region(n)[:, 0:F].rearrange("(m p) f -> p m f", p=P), in_=bds[n][:]
+            )
+
+        def fetch(n):
+            shf[n] = pool.tile([P, 2, WIN], F32, name="shf", bufs=3)
+            flat = region(n).rearrange("u c -> (u c)").rearrange("(m x) -> m x", m=2)
+            skew = flat[:, 0 : P * (K - 1)].rearrange("m (p c) -> p m c", c=K - 1)
+            nc.sync.dma_start(out=shf[n][:], in_=skew[:, :, 0:WIN])
+
+        def mm_ac(n):
+            for m in range(2):
+                acb[n, m] = psum.tile([P, K], F32, name="ac", bufs=3)
+                mm(acb[n, m][:], n, m, kcod[n], kscl[n], K)
+
+        def add(n, m):
+            if m == 0:
+                res[n] = pool.tile([P, 2, K], F32, name="res", bufs=3)
+            ac = acb[n, m][:].rearrange("q (i p) -> q p i", i=4)
+            rv = res[n][:, m, :].rearrange("q (p i) -> q p i", i=4)
+            lo = 32 * m
+            nc.vector.tensor_tensor(
+                out=rv[:, lo : lo + 96, :],
+                in0=ac[:, lo : lo + 96, :],
+                in1=shf[n][:, m, :].rearrange("q (p i) -> q p i", i=4),
+                op=ADD,
+            )
+            r0 = 96 if m == 0 else 0
+            nc.scalar.copy(out=rv[:, r0 : r0 + 32, :], in_=ac[:, r0 : r0 + 32, :])
+
+        def store(n, m):
+            b, w = blk(n)
+            nc.sync.dma_start(out=out[b, 0, w][P * m : P * (m + 1), :], in_=res[n][:, m, :])
+
+        with tc.manual_schedule():
+            nc.sync.dma_start(
+                out=scale[:],
+                in_=keys_scale.rearrange("a b c d k -> (a b c d k)").partition_broadcast(P),
+            )
+            load_k(0)
+            load_w(0)
+            nc.sync.dma_start(
+                out=s_raw[:].rearrange("p (j k) -> p j k", j=2),
+                in_=sin_emb.rearrange("(j p) k -> p j k", p=P),
+            )
+            load_w(1)
+            load_k(1)
+            load_w(2)
+            load_w(3)
+            load_q(0)
+            load_q(1)
+            load_k(2)
+
+            prod(0, 0)
+            do_w(0)
+            prod(0, 1)
+            do_sin()
+            prod(0, 2)
+            do_w(1)
+            prod(0, 3)
+            do_w(2)
+            do_w(3)
+            for i in range(4):
+                transp_k(0, i)
+                if i % 2:
+                    copy_k(0, i // 2)
+            transp_q(0)
+            for r in range(NSCR):
+                nc.sync.dma_start(
+                    out=region(r)[:, F:K].rearrange("(m p) f -> p m f", p=P), in_=zeros[:]
+                )
+            load_q(2)
+
+            load_k(3)
+            load_q(3)
+            for i in range(4):
+                prod(1, i)
+            quant(s_cod[:], s_scl[:], s_grp[:])
+            for c in range(4):
+                quant_w(c)
+            for G in range(2):
+                for fh in range(2):
+                    proj(G, fh)
+            quant_k(0, 0)
+            quant_k(0, 1)
+            quant_q(0)
+            for i in range(4):
+                transp_k(1, i)
+                if i % 2:
+                    copy_k(1, i // 2)
+            transp_q(1)
+
+            for n in range(2, NB + ADD_LAG):
+                if 2 <= n and n + 2 < NB and n + 2 > 3:
+                    load_k(n + 2)
+                    load_q(n + 2)
+                if n > 2 and n - 1 < NB:
+                    fetch(n - 1)
+                live = n < NB
+                if live:
+                    prod(n, 0)
+                    transp_q(n)
+                    transp_k(n, 0)
+                    prod(n, 1)
+                    transp_k(n, 1)
+                    copy_k(n, 0)
+                if n == 2:
+                    quant(p_cod[:], p_scl[:], p_grp[:])
+                    mm_bd(0)
+                    park(0)
+                    fetch(0)
+                if n - ADD_LAG >= 0:
+                    add(n - ADD_LAG, 0)
+                    store(n - ADD_LAG, 0)
+                if n - 1 < NB:
+                    quant_k(n - 1, 0)
+                if live:
+                    prod(n, 2)
+                    transp_k(n, 2)
+                if n - 1 < NB:
+                    quant_k(n - 1, 1)
+                if 0 <= n - AC_LAG < NB:
+                    mm_ac(n - AC_LAG)
+                if n == 2:
+                    quant_q(1)
+                    mm_bd(1)
+                    park(1)
+                    fetch(1)
+                if live:
+                    prod(n, 3)
+                    transp_k(n, 3)
+                    copy_k(n, 1)
+                if n - ADD_LAG >= 0:
+                    add(n - ADD_LAG, 1)
+                    store(n - ADD_LAG, 1)
+                if live:
+                    quant_q(n)
+                    mm_bd(n)
+                    park(n)

@@ -16,20 +16,28 @@ ADD = mybir.AluOpType.add
 MULT = mybir.AluOpType.mult
 
 P = 128
-NB = B * W
-NSCR = 3
-WIN = 384
-AC_LAG = 2
-ADD_LAG = 3
+PASS = 512
+WORDS = PASS // 2
+BLOCKS = B * W
+LAST = BLOCKS - 1
+SCRATCH = 3
+REACH = 384
 
 
 def tile_gemma3naudiorelativepositionembedding_pa_t_kernel(
     tc, queries, keys_bytes, keys_scale, sin_emb, pos_w, out
 ):
     nc = tc.nc
+    scale_row = keys_scale.rearrange("a b c d k -> (a b c d k)")
 
-    def blk(n):
-        return n // W, n % W
+    def out_block(n):
+        return out[n // W, 0, n % W]
+
+    def scratch_block(n):
+        return out_block(LAST - (LAST - n) % SCRATCH)
+
+    def key_rows(n):
+        return keys_bytes[n // W, n % W].rearrange("(p i) h k -> p i (h k)", i=4)
 
     with ExitStack() as ctx:
         keep = ctx.enter_context(tc.tile_pool(name="keep", bufs=1))
@@ -40,306 +48,320 @@ def tile_gemma3naudiorelativepositionembedding_pa_t_kernel(
         make_identity(nc, ident[:])
         zeros = keep.tile([P, 2, F], F32, name="zeros")
         nc.gpsimd.memset(zeros[:], 0.0)
-        scale = keep.tile([P, D], F32, name="scale")
+        scale = keep.tile([P, 2 * D], F32, name="scale")
+
         w_raw = keep.tile([P, 8 * D], BF16, name="w_raw")
         w_grp = keep.tile([P, 8 * D], BF16, name="w_grp", align_bytes=64)
-        w_cod = keep.tile([P, 4 * 512], U32, name="w_cod", align_bytes=64)
-        w_scl = keep.tile([P, 4 * 512], U8, name="w_scl", align_bytes=64)
+        w_cod = keep.tile([P, 8 * WORDS], U32, name="w_cod", align_bytes=64)
+        w_scl = keep.tile([P, 8 * WORDS], U8, name="w_scl", align_bytes=64)
         s_raw = keep.tile([P, 2 * D], BF16, name="s_raw")
         s_grp = keep.tile([P, 2 * D], BF16, name="s_grp", align_bytes=64)
-        s_cod = keep.tile([P, 512], U32, name="s_cod", align_bytes=64)
-        s_scl = keep.tile([P, 512], U8, name="s_scl", align_bytes=64)
+        s_cod = keep.tile([P, 2 * F], U32, name="s_cod", align_bytes=64)
+        s_scl = keep.tile([P, 2 * F], U8, name="s_scl", align_bytes=64)
         p_grp = keep.tile([P, 2 * D], BF16, name="p_grp", align_bytes=64)
-        p_cod = keep.tile([P, 512], U32, name="p_cod", align_bytes=64)
-        p_scl = keep.tile([P, 512], U8, name="p_scl", align_bytes=64)
+        p_cod = keep.tile([P, 2 * F], U32, name="p_cod", align_bytes=64)
+        p_scl = keep.tile([P, 2 * F], U8, name="p_scl", align_bytes=64)
 
-        kbytes, kval, kgrp, kcod, kscl = {}, {}, {}, {}, {}
-        qraw, qgrp, qcod, qscl = {}, {}, {}, {}
-        bank, acb, bdb, bds, shf, res = {}, {}, {}, {}, {}, {}
+        k_bytes, k_val, k_grp, k_cod, k_scl = {}, {}, {}, {}, {}
+        q_raw, q_grp, q_cod, q_scl = {}, {}, {}, {}
+        turned, bd, shifted, ac, res = {}, {}, {}, {}, {}
 
-        def load_k(n):
-            b, w = blk(n)
-            kbytes[n] = pool.tile([P, 4 * D], U8, name="kbytes", bufs=3)
-            nc.sync.dma_start(
-                out=kbytes[n][:],
-                in_=keys_bytes[b, w].rearrange("(p i) h k -> p (i h k)", i=4),
-            )
+        def load_scale(g):
+            cols = slice(PASS * g, PASS * (g + 1))
+            nc.sync.dma_start(out=scale[:, cols], in_=scale_row[cols].partition_broadcast(P))
 
-        def load_q(n):
-            b, w = blk(n)
-            qraw[n] = pool.tile([P, 2 * D], BF16, name="qraw", bufs=3)
-            nc.sync.dma_start(
-                out=qraw[n][:].rearrange("p (m k) -> p m k", m=2),
-                in_=queries[b, w].rearrange("(m p) h k -> p m (h k)", p=P),
-            )
-
-        def load_w(c):
-            g, t0 = c // 2, 2 * (c % 2)
-            nc.sync.dma_start(
-                out=w_raw[:, c * 2 * D : (c + 1) * 2 * D].rearrange("m (t k) -> m t k", t=2),
-                in_=pos_w[512 * g : 512 * (g + 1), :].rearrange("(m t) k -> m t k", t=4)[:, t0 : t0 + 2, :],
-            )
-
-        def transp(key, src, base, j):
-            words = src.bitcast(F32)
-            for g in range(2):
-                if j == 0:
-                    bank[key, g] = psum.tile([P, 2, 2, P], F32, name="tp", bufs=4)
-                for u in range(2):
-                    w0 = base // 2 + 256 * g
-                    nc.tensor.transpose(
-                        bank[key, g][:, j, u, :], words[:, w0 + u : w0 + 256 : 2], ident[:]
-                    )
-
-        def copy_out(key, g, dst):
-            nc.scalar.copy(
-                out=dst.bitcast(F32).rearrange("p (j r u) -> p j r u", j=2, u=2),
-                in_=bank.pop((key, g))[:].rearrange("p j u r -> p j r u"),
-            )
-
-        def quant(cod, scl, grp):
-            nc.vector.quantize_mx(out=cod.bitcast(FP8X4), scales=scl, in_=grp)
-
-        def do_sin():
-            transp("s", s_raw[:], 0, 0)
-            transp("s", s_raw[:], D, 1)
-            for g in range(2):
-                copy_out("s", g, s_grp[:, g * D : (g + 1) * D])
-
-        def do_w(c):
-            transp("w", w_raw[:], c * 2 * D, 0)
-            transp("w", w_raw[:], c * 2 * D + D, 1)
-            for g in range(2):
-                copy_out("w", g, w_grp[:, (2 * c + g) * D : (2 * c + g + 1) * D])
-
-        def quant_w(c):
-            quant(
-                w_cod[:, 512 * c : 512 * (c + 1)],
-                w_scl[:, 512 * c : 512 * (c + 1)],
-                w_grp[:, 2 * D * c : 2 * D * (c + 1)],
-            )
-
-        def proj(G, fh):
-            pb = psum.tile([P, 4, P], F32, name="ac", bufs=3)
-            for t in range(4):
-                c = 2 * G + t // 2
-                for g in range(2):
-                    l0 = 512 * c + 256 * g + P * (t % 2)
-                    r0 = 256 * g + P * fh
-                    nc.tensor.matmul_mx(
-                        out=pb[:, t, :],
-                        lhsT=w_cod[:, l0 : l0 + P].bitcast(FP8X4),
-                        lhsT_scale=w_scl[:, l0 : l0 + P],
-                        rhs=s_cod[:, r0 : r0 + P].bitcast(FP8X4),
-                        rhs_scale=s_scl[:, r0 : r0 + P],
-                        start=(g == 0),
-                        stop=(g == 1),
-                    )
-            d0 = (2 * G + fh) * 512
-            nc.scalar.copy(
-                out=p_grp[:, d0 : d0 + 512].rearrange("p (f t) -> p f t", t=4),
-                in_=pb[:].rearrange("p t f -> p f t"),
-            )
-
-        def prod(n, i):
-            if i == 0:
-                kval[n] = pool.tile([P, 4 * D], BF16, name="kval", bufs=3)
-            cols = slice(i * D, (i + 1) * D)
-            nc.vector.tensor_tensor(
-                out=kval[n][:, cols], in0=kbytes[n][:, cols].bitcast(FP8), in1=scale[:], op=MULT
-            )
-
-        def transp_k(n, i):
-            transp(("k", n, i // 2), kval[n][:], i * D, i % 2)
-
-        def copy_k(n, pair):
-            if pair == 0:
-                kgrp[n] = pool.tile([P, 4 * D], BF16, name="kgrp", bufs=2, align_bytes=64)
-            for g in range(2):
-                d0 = (2 * g + pair) * D
-                copy_out(("k", n, pair), g, kgrp[n][:, d0 : d0 + D])
-
-        def quant_k(n, g):
+        def load_first_keys(g):
             if g == 0:
-                kcod[n] = pool.tile([P, 2 * K], U32, name="kcod", bufs=3, align_bytes=64)
-                kscl[n] = pool.tile([P, 2 * K], U8, name="kscl", bufs=3, align_bytes=64)
-            c = slice(g * K, (g + 1) * K)
-            quant(kcod[n][:, c], kscl[n][:, c], kgrp[n][:, 2 * D * g : 2 * D * (g + 1)])
-
-        def transp_q(n):
-            transp(("q", n), qraw[n][:], 0, 0)
-            transp(("q", n), qraw[n][:], D, 1)
-            qgrp[n] = pool.tile([P, 2 * D], BF16, name="qgrp", bufs=3, align_bytes=64)
-            for g in range(2):
-                copy_out(("q", n), g, qgrp[n][:, g * D : (g + 1) * D])
-
-        def quant_q(n):
-            qcod[n] = pool.tile([P, 512], U32, name="qcod", bufs=4, align_bytes=64)
-            qscl[n] = pool.tile([P, 512], U8, name="qscl", bufs=4, align_bytes=64)
-            quant(qcod[n][:], qscl[n][:], qgrp[n][:])
-
-        def mm(dst, n, m, cod, scl, width):
-            for g in range(2):
-                l0 = 256 * g + P * m
-                r = slice(width * g, width * (g + 1))
-                nc.tensor.matmul_mx(
-                    out=dst,
-                    lhsT=qcod[n][:, l0 : l0 + P].bitcast(FP8X4),
-                    lhsT_scale=qscl[n][:, l0 : l0 + P],
-                    rhs=cod[:, r].bitcast(FP8X4),
-                    rhs_scale=scl[:, r],
-                    start=(g == 0),
-                    stop=(g == 1),
-                )
-
-        def region(n):
-            b, w = blk(NB - 1 - (NB - 1 - n) % NSCR)
-            return out[b, 0, w]
-
-        def mm_bd(n):
-            bdb[n] = psum.tile([P, 2, F], F32, name="bd", bufs=1)
-            for m in range(2):
-                mm(bdb[n][:, m, :], n, m, p_cod, p_scl, F)
-            bds[n] = pool.tile([P, 2, F], F32, name="bds", bufs=3)
-            nc.scalar.copy(out=bds[n][:], in_=bdb[n][:])
-
-        def park(n):
+                k_bytes[0] = pool.tile([P, 4 * D], U8, name="k_bytes")
             nc.sync.dma_start(
-                out=region(n)[:, 0:F].rearrange("(m p) f -> p m f", p=P), in_=bds[n][:]
+                out=k_bytes[0][:, 2 * D * g : 2 * D * (g + 1)].rearrange("p (i k) -> p i k", i=4),
+                in_=key_rows(0)[:, :, PASS * g : PASS * (g + 1)],
             )
 
-        def fetch(n):
-            shf[n] = pool.tile([P, 2, WIN], F32, name="shf", bufs=3)
-            flat = region(n).rearrange("u c -> (u c)").rearrange("(m x) -> m x", m=2)
-            skew = flat[:, 0 : P * (K - 1)].rearrange("m (p c) -> p m c", c=K - 1)
-            nc.sync.dma_start(out=shf[n][:], in_=skew[:, :, 0:WIN])
+        def load_keys(n):
+            k_bytes[n] = pool.tile([P, 4 * D], U8, name="k_bytes")
+            nc.sync.dma_start(out=k_bytes[n][:], in_=key_rows(n).rearrange("p i k -> p (i k)"))
 
-        def mm_ac(n):
-            for m in range(2):
-                acb[n, m] = psum.tile([P, K], F32, name="ac", bufs=3)
-                mm(acb[n, m][:], n, m, kcod[n], kscl[n], K)
-
-        def add(n, m):
-            if m == 0:
-                res[n] = pool.tile([P, 2, K], F32, name="res", bufs=3)
-            ac = acb[n, m][:].rearrange("q (i p) -> q p i", i=4)
-            rv = res[n][:, m, :].rearrange("q (p i) -> q p i", i=4)
-            lo = 32 * m
-            nc.vector.tensor_tensor(
-                out=rv[:, lo : lo + 96, :],
-                in0=ac[:, lo : lo + 96, :],
-                in1=shf[n][:, m, :].rearrange("q (p i) -> q p i", i=4),
-                op=ADD,
-            )
-            r0 = 96 if m == 0 else 0
-            nc.scalar.copy(out=rv[:, r0 : r0 + 32, :], in_=ac[:, r0 : r0 + 32, :])
-
-        def store(n, m):
-            b, w = blk(n)
-            nc.sync.dma_start(out=out[b, 0, w][P * m : P * (m + 1), :], in_=res[n][:, m, :])
-
-        with tc.manual_schedule():
+        def load_queries(n):
+            q_raw[n] = pool.tile([P, 2 * D], BF16, name="q_raw")
             nc.sync.dma_start(
-                out=scale[:],
-                in_=keys_scale.rearrange("a b c d k -> (a b c d k)").partition_broadcast(P),
+                out=q_raw[n][:].rearrange("p (m k) -> p m k", m=2),
+                in_=queries[n // W, n % W].rearrange("(m p) h k -> p m (h k)", p=P),
             )
-            load_k(0)
-            load_w(0)
+
+        def load_sin():
             nc.sync.dma_start(
                 out=s_raw[:].rearrange("p (j k) -> p j k", j=2),
                 in_=sin_emb.rearrange("(j p) k -> p j k", p=P),
             )
+
+        def load_w(c):
+            t0 = 2 * (c % 2)
+            group = pos_w[PASS * (c // 2) : PASS * (c // 2 + 1), :].rearrange("(m t) k -> m t k", t=4)
+            nc.sync.dma_start(
+                out=w_raw[:, 2 * D * c : 2 * D * (c + 1)].rearrange("m (t k) -> m t k", t=2),
+                in_=group[:, t0 : t0 + 2, :],
+            )
+
+        def clear_scratch():
+            for n in range(SCRATCH):
+                nc.sync.dma_start(
+                    out=scratch_block(n)[:, F:K].rearrange("(m p) f -> p m f", p=P), in_=zeros[:]
+                )
+
+        def turn_tile(name, j, rows, starts):
+            words = rows.bitcast(F32)
+            for g in range(2):
+                if j == 0:
+                    turned[name, g] = psum.tile([P, 2, 2, P], F32, name="turned", bufs=4)
+                w0 = starts[g] // 2
+                for u in range(2):
+                    nc.tensor.transpose(
+                        turned[name, g][:, j, u, :], words[:, w0 + u : w0 + WORDS : 2], ident[:]
+                    )
+
+        def copy_turned(name, g, dst):
+            nc.scalar.copy(
+                out=dst.bitcast(F32).rearrange("p (j r u) -> p j r u", j=2, u=2),
+                in_=turned.pop((name, g))[:].rearrange("p j u r -> p j r u"),
+            )
+
+        def turn_couple(name, rows, c0, grp, d0):
+            for j in range(2):
+                turn_tile(name, j, rows, (c0 + D * j, c0 + D * j + PASS))
+            for g in range(2):
+                copy_turned(name, g, grp[:, d0 + D * g : d0 + D * (g + 1)])
+
+        def quantize(cod, scl, grp):
+            nc.vector.quantize_mx(out=cod.bitcast(FP8X4), scales=scl, in_=grp)
+
+        def multiply(dst, lhs, l0, rhs, r0, width):
+            for g in range(2):
+                lc, rc = slice(l0[g], l0[g] + P), slice(r0[g], r0[g] + width)
+                nc.tensor.matmul_mx(
+                    out=dst,
+                    lhsT=lhs[0][:, lc].bitcast(FP8X4),
+                    lhsT_scale=lhs[1][:, lc],
+                    rhs=rhs[0][:, rc].bitcast(FP8X4),
+                    rhs_scale=rhs[1][:, rc],
+                    start=(g == 0),
+                    stop=(g == 1),
+                )
+
+        def turn_sin():
+            turn_couple("s", s_raw[:], 0, s_grp, 0)
+
+        def turn_w(c):
+            turn_couple("w", w_raw[:], 2 * D * c, w_grp, 2 * D * c)
+
+        def quantize_w(c):
+            cols = slice(2 * WORDS * c, 2 * WORDS * (c + 1))
+            quantize(w_cod[:, cols], w_scl[:, cols], w_grp[:, 2 * D * c : 2 * D * (c + 1)])
+
+        def project(G, fh):
+            bank = psum.tile([P, 4, P], F32, name="ac", bufs=3)
+            for t in range(4):
+                l0 = 2 * WORDS * (2 * G + t // 2) + P * (t % 2)
+                multiply(
+                    bank[:, t, :], (w_cod, w_scl), (l0, l0 + WORDS), (s_cod, s_scl), (P * fh, F + P * fh), P
+                )
+            d0 = PASS * (2 * G + fh)
+            nc.scalar.copy(
+                out=p_grp[:, d0 : d0 + PASS].rearrange("p (f t) -> p f t", t=4),
+                in_=bank[:].rearrange("p t f -> p f t"),
+            )
+
+        def scale_keys(n, c0, width):
+            if c0 == 0:
+                k_val[n] = pool.tile([P, 4 * D], BF16, name="k_val")
+            cols = slice(c0, c0 + width)
+            s0 = PASS * (c0 // (2 * D)) if n == 0 else 0
+            nc.vector.tensor_tensor(
+                out=k_val[n][:, cols],
+                in0=k_bytes[n][:, cols].bitcast(FP8),
+                in1=scale[:, s0 : s0 + width],
+                op=MULT,
+            )
+
+        def turn_keys(n, couple):
+            if couple == 0:
+                k_grp[n] = pool.tile([P, 4 * D], BF16, name="k_grp", bufs=2, align_bytes=64)
+            for j in range(2):
+                i = 2 * couple + j
+                starts = (PASS * i, 2 * D + PASS * i) if n == 0 else (D * i, D * i + PASS)
+                turn_tile(("k", n), j, k_val[n][:], starts)
+            for g in range(2):
+                d0 = D * (2 * g + couple)
+                copy_turned(("k", n), g, k_grp[n][:, d0 : d0 + D])
+
+        def quantize_keys(n, calls):
+            k_cod[n] = pool.tile([P, 2 * K], U32, name="k_cod", align_bytes=64)
+            k_scl[n] = pool.tile([P, 2 * K], U8, name="k_scl", align_bytes=64)
+            step = 2 * K // calls
+            for h in range(calls):
+                cols = slice(step * h, step * (h + 1))
+                quantize(
+                    k_cod[n][:, cols], k_scl[n][:, cols], k_grp[n][:, 4 * step * h : 4 * step * (h + 1)]
+                )
+
+        def turn_queries(n):
+            q_grp[n] = pool.tile([P, 2 * D], BF16, name="q_grp", align_bytes=64)
+            turn_couple(("q", n), q_raw[n][:], 0, q_grp[n], 0)
+
+        def quantize_queries(n):
+            q_cod[n] = pool.tile([P, 2 * U], U32, name="q_cod", bufs=5, align_bytes=64)
+            q_scl[n] = pool.tile([P, 2 * U], U8, name="q_scl", bufs=5, align_bytes=64)
+            quantize(q_cod[n][:], q_scl[n][:], q_grp[n][:])
+
+        def query_product(dst, n, m, rhs, width):
+            multiply(dst, (q_cod[n], q_scl[n]), (P * m, U + P * m), rhs, (0, width), width)
+
+        def make_bd(n):
+            bank = psum.tile([P, 2, F], F32, name="bd", bufs=1)
+            for m in range(2):
+                query_product(bank[:, m, :], n, m, (p_cod, p_scl), F)
+            bd[n] = pool.tile([P, 2, F], F32, name="bd_rows")
+            nc.scalar.copy(out=bd[n][:], in_=bank[:])
+
+        def park_bd(n):
+            nc.sync.dma_start(
+                out=scratch_block(n)[:, 0:F].rearrange("(m p) f -> p m f", p=P), in_=bd[n][:]
+            )
+
+        def fetch_shifted(n):
+            shifted[n] = pool.tile([P, 2, REACH], F32, name="shifted")
+            flat = scratch_block(n).rearrange("u c -> (u c)").rearrange("(m x) -> m x", m=2)
+            skew = flat[:, 0 : P * (K - 1)].rearrange("m (p c) -> p m c", c=K - 1)
+            nc.sync.dma_start(out=shifted[n][:], in_=skew[:, :, 0:REACH])
+
+        def make_ac(n, m):
+            ac[n, m] = psum.tile([P, K], F32, name="ac", bufs=3)
+            query_product(ac[n, m][:], n, m, (k_cod[n], k_scl[n]), K)
+            if m == 0:
+                res[n] = pool.tile([P, 2, K], F32, name="res")
+            r0 = 96 if m == 0 else 0
+            nc.scalar.copy(
+                out=res[n][:, m, :].rearrange("q (r i) -> q r i", i=4)[:, r0 : r0 + 32, :],
+                in_=ac[n, m][:].rearrange("q (i r) -> q r i", i=4)[:, r0 : r0 + 32, :],
+            )
+
+        def finish(n, m):
+            r0 = 32 * m
+            nc.vector.tensor_tensor(
+                out=res[n][:, m, :].rearrange("q (r i) -> q r i", i=4)[:, r0 : r0 + 96, :],
+                in0=ac[n, m][:].rearrange("q (i r) -> q r i", i=4)[:, r0 : r0 + 96, :],
+                in1=shifted[n][:, m, :].rearrange("q (r i) -> q r i", i=4),
+                op=ADD,
+            )
+            nc.sync.dma_start(out=out_block(n)[P * m : P * (m + 1), :], in_=res[n][:, m, :])
+
+        with tc.manual_schedule():
+            load_scale(0)
+            load_first_keys(0)
+            load_w(0)
+            load_scale(1)
+            load_first_keys(1)
             load_w(1)
-            load_k(1)
+            load_sin()
+            load_keys(1)
             load_w(2)
             load_w(3)
-            load_q(0)
-            load_q(1)
-            load_k(2)
+            load_queries(0)
+            load_keys(2)
+            load_queries(1)
 
-            prod(0, 0)
-            do_w(0)
-            prod(0, 1)
-            do_sin()
-            prod(0, 2)
-            do_w(1)
-            prod(0, 3)
-            do_w(2)
-            do_w(3)
+            turn_w(0)
             for i in range(4):
-                transp_k(0, i)
-                if i % 2:
-                    copy_k(0, i // 2)
-            transp_q(0)
-            for r in range(NSCR):
-                nc.sync.dma_start(
-                    out=region(r)[:, F:K].rearrange("(m p) f -> p m f", p=P), in_=zeros[:]
-                )
-            load_q(2)
-
-            load_k(3)
-            load_q(3)
-            for i in range(4):
-                prod(1, i)
-            quant(s_cod[:], s_scl[:], s_grp[:])
-            for c in range(4):
-                quant_w(c)
+                scale_keys(0, PASS * i, PASS)
+            turn_w(1)
+            for i in range(4, 8):
+                scale_keys(0, PASS * i, PASS)
+            turn_sin()
+            turn_w(2)
+            quantize_w(0)
+            scale_keys(1, 0, D)
+            scale_keys(1, D, D)
+            turn_w(3)
+            nc.scalar.copy(out=scale[:, D : 2 * D], in_=scale[:, 0:D])
+            quantize(s_cod[:], s_scl[:], s_grp[:])
+            quantize_w(1)
+            quantize_w(2)
+            scale_keys(1, 2 * D, D)
+            scale_keys(1, 3 * D, D)
+            quantize_w(3)
+            turn_keys(0, 0)
             for G in range(2):
                 for fh in range(2):
-                    proj(G, fh)
-            quant_k(0, 0)
-            quant_k(0, 1)
-            quant_q(0)
-            for i in range(4):
-                transp_k(1, i)
-                if i % 2:
-                    copy_k(1, i // 2)
-            transp_q(1)
+                    project(G, fh)
+            turn_keys(0, 1)
+            turn_queries(0)
+            turn_queries(1)
+            scale_keys(2, 0, 2 * D)
+            clear_scratch()
+            load_queries(2)
+            load_keys(3)
+            load_queries(3)
+            load_keys(4)
+            quantize(p_cod[:], p_scl[:], p_grp[:])
+            scale_keys(2, 2 * D, 2 * D)
+            quantize_queries(0)
+            make_bd(0)
+            park_bd(0)
+            quantize_queries(1)
 
-            for n in range(2, NB + ADD_LAG):
-                if 2 <= n and n + 2 < NB and n + 2 > 3:
-                    load_k(n + 2)
-                    load_q(n + 2)
-                if n > 2 and n - 1 < NB:
-                    fetch(n - 1)
-                live = n < NB
-                if live:
-                    prod(n, 0)
-                    transp_q(n)
-                    transp_k(n, 0)
-                    prod(n, 1)
-                    transp_k(n, 1)
-                    copy_k(n, 0)
-                if n == 2:
-                    quant(p_cod[:], p_scl[:], p_grp[:])
-                    mm_bd(0)
-                    park(0)
-                    fetch(0)
-                if n - ADD_LAG >= 0:
-                    add(n - ADD_LAG, 0)
-                    store(n - ADD_LAG, 0)
-                if n - 1 < NB:
-                    quant_k(n - 1, 0)
-                if live:
-                    prod(n, 2)
-                    transp_k(n, 2)
-                if n - 1 < NB:
-                    quant_k(n - 1, 1)
-                if 0 <= n - AC_LAG < NB:
-                    mm_ac(n - AC_LAG)
-                if n == 2:
-                    quant_q(1)
-                    mm_bd(1)
-                    park(1)
-                    fetch(1)
-                if live:
-                    prod(n, 3)
-                    transp_k(n, 3)
-                    copy_k(n, 1)
-                if n - ADD_LAG >= 0:
-                    add(n - ADD_LAG, 1)
-                    store(n - ADD_LAG, 1)
-                if live:
-                    quant_q(n)
-                    mm_bd(n)
-                    park(n)
+            products = [(n, 2 * D * h, 2 * D) for n in range(3, BLOCKS) for h in range(2)]
+            products[-1:] = [(LAST, 2 * D, D), (LAST, 3 * D, D)]
+
+            def next_products(count):
+                for product in products[:count]:
+                    scale_keys(*product)
+                products[:count] = []
+
+            for n in range(1, BLOCKS):
+                final = n == LAST
+                if n + 4 < BLOCKS:
+                    load_keys(n + 4)
+                if n + 3 < BLOCKS:
+                    load_queries(n + 3)
+                next_products(1)
+                if final:
+                    make_bd(n)
+                    park_bd(n)
+                else:
+                    turn_queries(n + 1)
+                if n >= 2:
+                    make_ac(n - 2, 0)
+                if n >= 3:
+                    finish(n - 3, 0)
+                fetch_shifted(n - 1)
+                turn_keys(n, 0)
+                if final:
+                    fetch_shifted(n)
+                else:
+                    make_bd(n)
+                    park_bd(n)
+                quantize_keys(n - 1, 1)
+                if final:
+                    make_ac(n - 2, 1)
+                    finish(n - 3, 1)
+                if n % 3 != 2 or n == 2:
+                    next_products(2 if final else 1)
+                turn_keys(n, 1)
+                if not final and n >= 2:
+                    make_ac(n - 2, 1)
+                if not final and n >= 3:
+                    finish(n - 3, 1)
+                if not final:
+                    quantize_queries(n + 1)
+
+            make_ac(LAST - 1, 0)
+            finish(LAST - 2, 0)
+            make_ac(LAST - 1, 1)
+            finish(LAST - 2, 1)
+            finish(LAST - 1, 0)
+            quantize_keys(LAST, 2)
+            finish(LAST - 1, 1)
+            for m in range(2):
+                make_ac(LAST, m)
+            for m in range(2):
+                finish(LAST, m)

from contextlib import ExitStack

import concourse.mybir as mybir
from concourse.masks import make_identity

B, W, U, D, K, F = 2, 8, 256, 1024, 512, 256
FLOPS = 2 * (B * W * U * K * D + B * W * U * F * D + F * D * D)

F32 = mybir.dt.float32
BF16 = mybir.dt.bfloat16
U32 = mybir.dt.uint32
U8 = mybir.dt.uint8
FP8 = mybir.dt.float8_e4m3fn
FP8X4 = mybir.dt.float8_e4m3fn_x4
ADD = mybir.AluOpType.add
MULT = mybir.AluOpType.mult

P = 128
PASS = 512
WORDS = PASS // 2
BLOCKS = B * W
LAST = BLOCKS - 1
SCRATCH = 3
REACH = 384


def tile_gemma3naudiorelativepositionembedding_pa_t_kernel(
    tc, queries, keys_bytes, keys_scale, sin_emb, pos_w, out
):
    nc = tc.nc
    scale_row = keys_scale.rearrange("a b c d k -> (a b c d k)")

    def out_block(n):
        return out[n // W, 0, n % W]

    def scratch_block(n):
        return out_block(LAST - (LAST - n) % SCRATCH)

    def key_rows(n):
        return keys_bytes[n // W, n % W].rearrange("(p i) h k -> p i (h k)", i=4)

    with ExitStack() as ctx:
        keep = ctx.enter_context(tc.tile_pool(name="keep", bufs=1))
        pool = ctx.enter_context(tc.tile_pool(name="pool", bufs=3))
        psum = ctx.enter_context(tc.psum_pool(name="psum", bufs=1))

        ident = keep.tile([P, P], F32, name="ident")
        make_identity(nc, ident[:])
        zeros = keep.tile([P, 2, F], F32, name="zeros")
        nc.gpsimd.memset(zeros[:], 0.0)
        scale = keep.tile([P, 2 * D], F32, name="scale")

        w_raw = keep.tile([P, 8 * D], BF16, name="w_raw")
        w_grp = keep.tile([P, 8 * D], BF16, name="w_grp", align_bytes=64)
        w_cod = keep.tile([P, 8 * WORDS], U32, name="w_cod", align_bytes=64)
        w_scl = keep.tile([P, 8 * WORDS], U8, name="w_scl", align_bytes=64)
        s_raw = keep.tile([P, 2 * D], BF16, name="s_raw")
        s_grp = keep.tile([P, 2 * D], BF16, name="s_grp", align_bytes=64)
        s_cod = keep.tile([P, 2 * F], U32, name="s_cod", align_bytes=64)
        s_scl = keep.tile([P, 2 * F], U8, name="s_scl", align_bytes=64)
        p_grp = keep.tile([P, 2 * D], BF16, name="p_grp", align_bytes=64)
        p_cod = keep.tile([P, 2 * F], U32, name="p_cod", align_bytes=64)
        p_scl = keep.tile([P, 2 * F], U8, name="p_scl", align_bytes=64)

        k_bytes, k_val, k_grp, k_cod, k_scl = {}, {}, {}, {}, {}
        q_raw, q_grp, q_cod, q_scl = {}, {}, {}, {}
        turned, bd, shifted, ac, res = {}, {}, {}, {}, {}

        def load_scale(g):
            cols = slice(PASS * g, PASS * (g + 1))
            nc.sync.dma_start(out=scale[:, cols], in_=scale_row[cols].partition_broadcast(P))

        def load_first_keys(g):
            if g == 0:
                k_bytes[0] = pool.tile([P, 4 * D], U8, name="k_bytes")
            nc.sync.dma_start(
                out=k_bytes[0][:, 2 * D * g : 2 * D * (g + 1)].rearrange("p (i k) -> p i k", i=4),
                in_=key_rows(0)[:, :, PASS * g : PASS * (g + 1)],
            )

        def load_keys(n):
            k_bytes[n] = pool.tile([P, 4 * D], U8, name="k_bytes")
            nc.sync.dma_start(out=k_bytes[n][:], in_=key_rows(n).rearrange("p i k -> p (i k)"))

        def load_queries(n):
            q_raw[n] = pool.tile([P, 2 * D], BF16, name="q_raw")
            nc.sync.dma_start(
                out=q_raw[n][:].rearrange("p (m k) -> p m k", m=2),
                in_=queries[n // W, n % W].rearrange("(m p) h k -> p m (h k)", p=P),
            )

        def load_sin():
            nc.sync.dma_start(
                out=s_raw[:].rearrange("p (j k) -> p j k", j=2),
                in_=sin_emb.rearrange("(j p) k -> p j k", p=P),
            )

        def load_w(c):
            t0 = 2 * (c % 2)
            group = pos_w[PASS * (c // 2) : PASS * (c // 2 + 1), :].rearrange("(m t) k -> m t k", t=4)
            nc.sync.dma_start(
                out=w_raw[:, 2 * D * c : 2 * D * (c + 1)].rearrange("m (t k) -> m t k", t=2),
                in_=group[:, t0 : t0 + 2, :],
            )

        def clear_scratch():
            for n in range(SCRATCH):
                nc.sync.dma_start(
                    out=scratch_block(n)[:, F:K].rearrange("(m p) f -> p m f", p=P), in_=zeros[:]
                )

        def turn_tile(name, j, rows, starts):
            words = rows.bitcast(F32)
            for g in range(2):
                if j == 0:
                    turned[name, g] = psum.tile([P, 2, 2, P], F32, name="turned", bufs=4)
                w0 = starts[g] // 2
                for u in range(2):
                    nc.tensor.transpose(
                        turned[name, g][:, j, u, :], words[:, w0 + u : w0 + WORDS : 2], ident[:]
                    )

        def copy_turned(name, g, dst):
            nc.scalar.copy(
                out=dst.bitcast(F32).rearrange("p (j r u) -> p j r u", j=2, u=2),
                in_=turned.pop((name, g))[:].rearrange("p j u r -> p j r u"),
            )

        def turn_couple(name, rows, c0, grp, d0):
            for j in range(2):
                turn_tile(name, j, rows, (c0 + D * j, c0 + D * j + PASS))
            for g in range(2):
                copy_turned(name, g, grp[:, d0 + D * g : d0 + D * (g + 1)])

        def quantize(cod, scl, grp):
            nc.vector.quantize_mx(out=cod.bitcast(FP8X4), scales=scl, in_=grp)

        def multiply(dst, lhs, l0, rhs, r0, width):
            for g in range(2):
                lc, rc = slice(l0[g], l0[g] + P), slice(r0[g], r0[g] + width)
                nc.tensor.matmul_mx(
                    out=dst,
                    lhsT=lhs[0][:, lc].bitcast(FP8X4),
                    lhsT_scale=lhs[1][:, lc],
                    rhs=rhs[0][:, rc].bitcast(FP8X4),
                    rhs_scale=rhs[1][:, rc],
                    start=(g == 0),
                    stop=(g == 1),
                )

        def turn_sin():
            turn_couple("s", s_raw[:], 0, s_grp, 0)

        def turn_w(c):
            turn_couple("w", w_raw[:], 2 * D * c, w_grp, 2 * D * c)

        def quantize_w(c):
            cols = slice(2 * WORDS * c, 2 * WORDS * (c + 1))
            quantize(w_cod[:, cols], w_scl[:, cols], w_grp[:, 2 * D * c : 2 * D * (c + 1)])

        def project(G, fh):
            bank = psum.tile([P, 4, P], F32, name="ac", bufs=3)
            for t in range(4):
                l0 = 2 * WORDS * (2 * G + t // 2) + P * (t % 2)
                multiply(
                    bank[:, t, :], (w_cod, w_scl), (l0, l0 + WORDS), (s_cod, s_scl), (P * fh, F + P * fh), P
                )
            d0 = PASS * (2 * G + fh)
            nc.scalar.copy(
                out=p_grp[:, d0 : d0 + PASS].rearrange("p (f t) -> p f t", t=4),
                in_=bank[:].rearrange("p t f -> p f t"),
            )

        def scale_keys(n, c0, width):
            if c0 == 0:
                k_val[n] = pool.tile([P, 4 * D], BF16, name="k_val")
            cols = slice(c0, c0 + width)
            s0 = PASS * (c0 // (2 * D)) if n == 0 else 0
            nc.vector.tensor_tensor(
                out=k_val[n][:, cols],
                in0=k_bytes[n][:, cols].bitcast(FP8),
                in1=scale[:, s0 : s0 + width],
                op=MULT,
            )

        def turn_keys(n, couple):
            if couple == 0:
                k_grp[n] = pool.tile([P, 4 * D], BF16, name="k_grp", bufs=2, align_bytes=64)
            for j in range(2):
                i = 2 * couple + j
                starts = (PASS * i, 2 * D + PASS * i) if n == 0 else (D * i, D * i + PASS)
                turn_tile(("k", n), j, k_val[n][:], starts)
            for g in range(2):
                d0 = D * (2 * g + couple)
                copy_turned(("k", n), g, k_grp[n][:, d0 : d0 + D])

        def quantize_keys(n, calls):
            k_cod[n] = pool.tile([P, 2 * K], U32, name="k_cod", align_bytes=64)
            k_scl[n] = pool.tile([P, 2 * K], U8, name="k_scl", align_bytes=64)
            step = 2 * K // calls
            for h in range(calls):
                cols = slice(step * h, step * (h + 1))
                quantize(
                    k_cod[n][:, cols], k_scl[n][:, cols], k_grp[n][:, 4 * step * h : 4 * step * (h + 1)]
                )

        def turn_queries(n):
            q_grp[n] = pool.tile([P, 2 * D], BF16, name="q_grp", align_bytes=64)
            turn_couple(("q", n), q_raw[n][:], 0, q_grp[n], 0)

        def quantize_queries(n):
            q_cod[n] = pool.tile([P, 2 * U], U32, name="q_cod", bufs=5, align_bytes=64)
            q_scl[n] = pool.tile([P, 2 * U], U8, name="q_scl", bufs=5, align_bytes=64)
            quantize(q_cod[n][:], q_scl[n][:], q_grp[n][:])

        def query_product(dst, n, m, rhs, width):
            multiply(dst, (q_cod[n], q_scl[n]), (P * m, U + P * m), rhs, (0, width), width)

        def make_bd(n):
            bank = psum.tile([P, 2, F], F32, name="bd", bufs=1)
            for m in range(2):
                query_product(bank[:, m, :], n, m, (p_cod, p_scl), F)
            bd[n] = pool.tile([P, 2, F], F32, name="bd_rows")
            nc.scalar.copy(out=bd[n][:], in_=bank[:])

        def park_bd(n):
            nc.sync.dma_start(
                out=scratch_block(n)[:, 0:F].rearrange("(m p) f -> p m f", p=P), in_=bd[n][:]
            )

        def fetch_shifted(n):
            shifted[n] = pool.tile([P, 2, REACH], F32, name="shifted")
            flat = scratch_block(n).rearrange("u c -> (u c)").rearrange("(m x) -> m x", m=2)
            skew = flat[:, 0 : P * (K - 1)].rearrange("m (p c) -> p m c", c=K - 1)
            nc.sync.dma_start(out=shifted[n][:], in_=skew[:, :, 0:REACH])

        def make_ac(n, m):
            ac[n, m] = psum.tile([P, K], F32, name="ac", bufs=3)
            query_product(ac[n, m][:], n, m, (k_cod[n], k_scl[n]), K)
            if m == 0:
                res[n] = pool.tile([P, 2, K], F32, name="res")
            r0 = 96 if m == 0 else 0
            nc.scalar.copy(
                out=res[n][:, m, :].rearrange("q (r i) -> q r i", i=4)[:, r0 : r0 + 32, :],
                in_=ac[n, m][:].rearrange("q (i r) -> q r i", i=4)[:, r0 : r0 + 32, :],
            )

        def finish(n, m):
            r0 = 32 * m
            nc.vector.tensor_tensor(
                out=res[n][:, m, :].rearrange("q (r i) -> q r i", i=4)[:, r0 : r0 + 96, :],
                in0=ac[n, m][:].rearrange("q (i r) -> q r i", i=4)[:, r0 : r0 + 96, :],
                in1=shifted[n][:, m, :].rearrange("q (r i) -> q r i", i=4),
                op=ADD,
            )
            nc.sync.dma_start(out=out_block(n)[P * m : P * (m + 1), :], in_=res[n][:, m, :])

        with tc.manual_schedule():
            load_scale(0)
            load_first_keys(0)
            load_w(0)
            load_scale(1)
            load_first_keys(1)
            load_w(1)
            load_sin()
            load_keys(1)
            load_w(2)
            load_w(3)
            load_queries(0)
            load_keys(2)
            load_queries(1)

            turn_w(0)
            for i in range(4):
                scale_keys(0, PASS * i, PASS)
            turn_w(1)
            for i in range(4, 8):
                scale_keys(0, PASS * i, PASS)
            turn_sin()
            turn_w(2)
            quantize_w(0)
            scale_keys(1, 0, D)
            scale_keys(1, D, D)
            turn_w(3)
            nc.scalar.copy(out=scale[:, D : 2 * D], in_=scale[:, 0:D])
            quantize(s_cod[:], s_scl[:], s_grp[:])
            quantize_w(1)
            quantize_w(2)
            scale_keys(1, 2 * D, D)
            scale_keys(1, 3 * D, D)
            quantize_w(3)
            turn_keys(0, 0)
            for G in range(2):
                for fh in range(2):
                    project(G, fh)
            turn_keys(0, 1)
            turn_queries(0)
            turn_queries(1)
            scale_keys(2, 0, 2 * D)
            clear_scratch()
            load_queries(2)
            load_keys(3)
            load_queries(3)
            load_keys(4)
            quantize(p_cod[:], p_scl[:], p_grp[:])
            scale_keys(2, 2 * D, 2 * D)
            quantize_queries(0)
            make_bd(0)
            park_bd(0)
            quantize_queries(1)

            products = [(n, 2 * D * h, 2 * D) for n in range(3, BLOCKS) for h in range(2)]
            products[-1:] = [(LAST, 2 * D, D), (LAST, 3 * D, D)]

            def next_products(count):
                for product in products[:count]:
                    scale_keys(*product)
                products[:count] = []

            for n in range(1, BLOCKS):
                final = n == LAST
                if n + 4 < BLOCKS:
                    load_keys(n + 4)
                if n + 3 < BLOCKS:
                    load_queries(n + 3)
                next_products(1)
                if final:
                    make_bd(n)
                    park_bd(n)
                else:
                    turn_queries(n + 1)
                if n >= 2:
                    make_ac(n - 2, 0)
                if n >= 3:
                    finish(n - 3, 0)
                fetch_shifted(n - 1)
                turn_keys(n, 0)
                if final:
                    fetch_shifted(n)
                else:
                    make_bd(n)
                    park_bd(n)
                quantize_keys(n - 1, 1)
                if final:
                    make_ac(n - 2, 1)
                    finish(n - 3, 1)
                if n % 3 != 2 or n == 2:
                    next_products(2 if final else 1)
                turn_keys(n, 1)
                if not final and n >= 2:
                    make_ac(n - 2, 1)
                if not final and n >= 3:
                    finish(n - 3, 1)
                if not final:
                    quantize_queries(n + 1)

            make_ac(LAST - 1, 0)
            finish(LAST - 2, 0)
            make_ac(LAST - 1, 1)
            finish(LAST - 2, 1)
            finish(LAST - 1, 0)
            quantize_keys(LAST, 2)
            finish(LAST - 1, 1)
            for m in range(2):
                make_ac(LAST, m)
            for m in range(2):
                finish(LAST, m)
